import numpy as np
import ml_dtypes


def mxq(x, axis, fmt="e4m3"):
    dtype, down = {"e4m3": (ml_dtypes.float8_e4m3fn, 7), "e5m2": (ml_dtypes.float8_e5m2, 14)}[fmt]
    v = np.moveaxis(np.asarray(x, np.float32).astype(ml_dtypes.bfloat16).astype(np.float64), axis, -1)
    blocks = v.reshape(v.shape[:-1] + (-1, 32))
    amax = np.abs(blocks).max(-1, keepdims=True)
    byte = np.maximum(np.where(amax > 0, np.frexp(amax)[1] - 1 + 127, 0) - down, 1)
    scale = np.exp2(byte - 127.0)
    codes = (blocks / scale).astype(np.float32).astype(dtype).astype(np.float64)
    return np.moveaxis((codes * scale).reshape(v.shape), -1, axis)


WIDE = False


def mx_kscale(k):
    if not WIDE:
        return np.ones(k)
    levels = np.array([10, -10, 5, -5, 0])
    a = np.random.permutation(np.resize(levels, k // 512 * 4)).reshape(k // 512, 4)
    idx = np.arange(k)
    return np.exp2(a[idx // 512, idx % 128 // 32])


BF16 = ml_dtypes.bfloat16


def bf(x):
    return np.asarray(x, np.float32).astype(BF16)


def f64(x):
    return np.asarray(x).astype(np.float64)


B, C, C8, H, W, S = 2, 1024, 256, 64, 64, 32
T = H * W
S2 = S * S
PH, PW = H // S, W // S


def setup_inputs():
    s = mx_kscale(C)
    return {"x": bf(np.random.standard_normal((B, C, H, W)) * s[None, :, None, None]),
            "Wq": bf(np.random.standard_normal((C8, C)) * 2.0 / np.sqrt(C) / s[None, :]),
            "bq": bf(np.random.standard_normal(C8) * 0.5),
            "Wk": bf(np.random.standard_normal((C8, C)) * 2.0 / np.sqrt(C) / s[None, :]),
            "bk": bf(np.random.standard_normal(C8) * 0.3)}


def reference(x, Wq, bq, Wk, bk):
    xq = mxq(f64(x).reshape(B, C, T), 1, "e4m3")
    qc = (mxq(f64(Wq), 1, "e4m3") @ xq) + f64(bq)[None, :, None]
    kc = (mxq(f64(Wk), 1, "e4m3") @ xq) + f64(bk)[None, :, None]
    q = qc.transpose(0, 2, 1)
    k_pool = kc.reshape(B, C8, S, PH, S, PW).mean(axis=(3, 5)).reshape(B, C8, S2)
    return q, k_pool

@@ -1,0 +1,234 @@
+from contextlib import ExitStack
+
+import concourse.mybir as mybir
+from concourse.masks import make_identity
+
+BF16 = mybir.dt.bfloat16
+F32 = mybir.dt.float32
+U32 = mybir.dt.uint32
+U8 = mybir.dt.uint8
+FP8X4 = mybir.dt.float8_e4m3fn_x4
+ADD = mybir.AluOpType.add
+MULT = mybir.AluOpType.mult
+IDENTITY = mybir.ActivationFunctionType.Identity
+
+B, C, C8, H, W = 2, 1024, 256, 64, 64
+P = 128
+PACK = 4
+PASSES = C // (P * PACK)
+SLAB_ROWS = 16
+SLAB_PX = SLAB_ROWS * W
+SLAB_PAIRS = SLAB_PX // 2
+SLABS_PER_IMAGE = H // SLAB_ROWS
+N_PIECES = B * SLABS_PER_IMAGE * PASSES
+N_UNITS = B * SLABS_PER_IMAGE * 2
+BLOCKS = 2
+RUN = 4
+RUNS = SLAB_PAIRS // RUN
+SCALAR_RUNS = 88
+RAW_BUFS = 8
+WQ, WK = 0, 1
+
+FLOPS = 2 * B * H * W * C * 2 * C8
+
+
+def tile_selfattention_pb_t_kernel(tc, x, Wq, bq, Wk, bk, out_0, out_1):
+    nc = tc.nc
+    x_view = x.rearrange("b (g p j) h w -> b g p j (h w)", g=PASSES, p=P, j=PACK)
+    q_view = out_0.rearrange(
+        "b (u k p d) o -> b u p k (d o)", u=2 * SLABS_PER_IMAGE, k=BLOCKS, p=P, d=2
+    )
+    k_view = out_1.rearrange("b (h o) t -> b h o t", h=2)
+
+    with ExitStack() as ctx:
+        const = ctx.enter_context(tc.tile_pool(name="const", bufs=1))
+        raw_pool = ctx.enter_context(tc.tile_pool(name="raw", bufs=RAW_BUFS))
+        grouped_pool = ctx.enter_context(tc.tile_pool(name="grouped", bufs=3))
+        codes_pool = ctx.enter_context(tc.tile_pool(name="codes", bufs=6))
+        q_stage_pool = ctx.enter_context(tc.tile_pool(name="q_stage", bufs=8))
+        k_stage_pool = ctx.enter_context(tc.tile_pool(name="k_stage", bufs=4))
+        even_pool = ctx.enter_context(tc.tile_pool(name="even", bufs=2))
+        setup_psum = ctx.enter_context(tc.psum_pool(name="setup_psum", bufs=2))
+        q_psum = ctx.enter_context(tc.psum_pool(name="q_psum", bufs=2 * BLOCKS))
+        k_psum = ctx.enter_context(tc.psum_pool(name="k_psum", bufs=2))
+
+        raw_tiles = {}
+        grouped_tiles = {}
+        x_codes = {}
+        x_scales = {}
+        q_banks = {}
+        k_banks = {}
+        k_stages = {}
+
+        def load(n):
+            slab, g = divmod(n, PASSES)
+            b, s = divmod(slab, SLABS_PER_IMAGE)
+            raw = raw_pool.tile([P, PACK, SLAB_PX], BF16)
+            nc.sync.dma_start(
+                out=raw[:], in_=x_view[b, g, :, :, s * SLAB_PX : (s + 1) * SLAB_PX]
+            )
+            raw_tiles[n] = raw
+
+        def regroup(n):
+            src = raw_tiles[n][:].rearrange("p j (c i d) -> p d c j i", i=RUN, d=2)
+            grouped = grouped_pool.tile([P, 2, SLAB_PAIRS, PACK], BF16, align_bytes=64)
+            dst = grouped[:].rearrange("p d (c i) j -> p d c j i", i=RUN)
+            for d in range(2):
+                nc.scalar.copy(out=dst[:, d, :SCALAR_RUNS], in_=src[:, d, :SCALAR_RUNS])
+                nc.vector.tensor_copy(out=dst[:, d, SCALAR_RUNS:], in_=src[:, d, SCALAR_RUNS:])
+            grouped_tiles[n] = grouped
+            if n + RAW_BUFS < N_PIECES:
+                load(n + RAW_BUFS)
+
+        def quantise(n):
+            codes = codes_pool.tile([P, 2 * SLAB_PAIRS], U32, align_bytes=64)
+            scales = codes_pool.tile([P, 2 * SLAB_PAIRS], U8, align_bytes=64)
+            nc.vector.quantize_mx(
+                out=codes[:].bitcast(FP8X4),
+                scales=scales[:],
+                in_=grouped_tiles[n][:].rearrange("p d q j -> p (d q j)"),
+            )
+            x_codes[n] = codes
+            x_scales[n] = scales
+
+        def prepare_weights():
+            w_words = w_rows[:].bitcast(F32).rearrange(
+                "o (w h g p u) -> o w h g u p", w=2, h=2, g=PASSES, p=P, u=2
+            )
+            grouped_words = w_grouped[:].bitcast(F32).rearrange(
+                "p (w g o u) -> p w g o u", w=2, g=PASSES, o=C8, u=2
+            )
+            for w in range(2):
+                for g in range(PASSES):
+                    planes = setup_psum.tile([P, 2, C8], F32, tag="setup")
+                    for u in range(2):
+                        for h in range(2):
+                            nc.tensor.transpose(
+                                planes[:, u, h * P : (h + 1) * P], w_words[:, w, h, g, u, :], ident[:]
+                            )
+                    nc.scalar.copy(
+                        out=grouped_words[:, w, g], in_=planes[:].rearrange("p u o -> p o u")
+                    )
+            nc.vector.quantize_mx(
+                out=w_codes[:].bitcast(FP8X4), scales=w_scales[:], in_=w_grouped[:]
+            )
+            spread = setup_psum.tile([P, C8 + 2 * 32], F32, tag="setup")
+            nc.tensor.matmul(
+                out=spread[:, :C8], lhsT=ones[:], rhs=bias_rows[:, :C8], start=True, stop=True
+            )
+            for h in range(2):
+                nc.tensor.matmul(
+                    out=spread[:, C8 + 32 * h : C8 + 32 * (h + 1)],
+                    lhsT=bias_rows[:, C8 + h * P : C8 + (h + 1) * P],
+                    rhs=ones[:, :32],
+                    start=True,
+                    stop=True,
+                )
+            nc.vector.tensor_copy(out=bias_q[:], in_=spread[:, :C8])
+            nc.vector.tensor_copy(
+                out=bias_k[:], in_=spread[:, C8:].rearrange("p (h n) -> p h n", h=2)[:, :, 0]
+            )
+
+        def multiply(unit):
+            slab, half = divmod(unit, 2)
+            pieces = [slab * PASSES + g for g in range(PASSES)]
+            q_banks[unit] = []
+            for k in range(BLOCKS):
+                q_ps = q_psum.tile([P, 2, C8], F32)
+                for d in range(2):
+                    first = d * SLAB_PAIRS + (half * BLOCKS + k) * P
+                    for g in range(PASSES):
+                        nc.tensor.matmul_mx(
+                            out=q_ps[:, d, :],
+                            lhsT=x_codes[pieces[g]][:, first : first + P].bitcast(FP8X4),
+                            lhsT_scale=x_scales[pieces[g]][:, first : first + P],
+                            rhs=w_codes_view[:, WQ, g, :].bitcast(FP8X4),
+                            rhs_scale=w_scales_view[:, WQ, g, :],
+                            start=(g == 0),
+                            stop=(g == PASSES - 1),
+                        )
+                q_banks[unit].append(q_ps)
+            k_ps = k_psum.tile([P, SLAB_PAIRS], F32)
+            for d in range(2):
+                for g in range(PASSES):
+                    nc.tensor.matmul_mx(
+                        out=k_ps[:],
+                        lhsT=w_codes_view[:, WK, g, half * P : (half + 1) * P].bitcast(FP8X4),
+                        lhsT_scale=w_scales_view[:, WK, g, half * P : (half + 1) * P],
+                        rhs=x_codes[pieces[g]][:, d * SLAB_PAIRS : (d + 1) * SLAB_PAIRS].bitcast(FP8X4),
+                        rhs_scale=x_scales[pieces[g]][:, d * SLAB_PAIRS : (d + 1) * SLAB_PAIRS],
+                        start=(d == 0 and g == 0),
+                        stop=(d == 1 and g == PASSES - 1),
+                    )
+            k_banks[unit] = k_ps
+
+        def evacuate(unit):
+            slab, half = divmod(unit, 2)
+            b, s = divmod(slab, SLABS_PER_IMAGE)
+            rows = k_banks[unit][:].rearrange("o (m e n) -> o e m n", e=2, n=W // 2)
+            even = even_pool.tile([P, SLAB_ROWS // 2, W // 2], F32)
+            nc.scalar.activation(
+                out=even[:], in_=rows[:, 0], func=IDENTITY, bias=bias_k[:, half : half + 1], scale=0.25
+            )
+            q_stage = q_stage_pool.tile([P, BLOCKS, 2, C8], F32)
+            for k in range(BLOCKS):
+                nc.vector.tensor_tensor(
+                    out=q_stage[:, k],
+                    in0=q_banks[unit][k][:],
+                    in1=bias_q[:].unsqueeze(1).to_broadcast([P, 2, C8]),
+                    op=ADD,
+                )
+            nc.sync.dma_start(
+                out=q_view[b, s * 2 + half], in_=q_stage[:].rearrange("p k d o -> p k (d o)")
+            )
+            if s == 0:
+                k_stage = k_stage_pool.tile([P, SLABS_PER_IMAGE, SLAB_ROWS // 2, W // 2], F32)
+                k_stages[(b, half)] = k_stage
+            nc.vector.scalar_tensor_tensor(
+                out=k_stages[(b, half)][:, s],
+                in0=rows[:, 1],
+                scalar=0.25,
+                in1=even[:],
+                op0=MULT,
+                op1=ADD,
+            )
+            if s == SLABS_PER_IMAGE - 1:
+                nc.sync.dma_start(
+                    out=k_view[b, half], in_=k_stages[(b, half)][:].rearrange("o s m n -> o (s m n)")
+                )
+
+        w_rows = const.tile([P, 2 * 2 * C], BF16)
+        w_grouped = const.tile([P, 2 * PASSES * C8 * PACK], BF16, align_bytes=64)
+        w_codes = const.tile([P, 2 * PASSES * C8], U32, align_bytes=64)
+        w_scales = const.tile([P, 2 * PASSES * C8], U8, align_bytes=64)
+        w_codes_view = w_codes[:].rearrange("p (w g o) -> p w g o", w=2, g=PASSES)
+        w_scales_view = w_scales[:].rearrange("p (w g o) -> p w g o", w=2, g=PASSES)
+        bias_rows = const.tile([P, 2 * C8], BF16)
+        bias_q = const.tile([P, C8], F32)
+        bias_k = const.tile([P, 2], F32)
+        ones = const.tile([P, P], BF16)
+        ident = const.tile([P, P], F32)
+
+        load(0)
+        w_rows_view = w_rows[:].rearrange("o (w h c) -> o w h c", w=2, h=2)
+        nc.sync.dma_start(out=w_rows_view[:, WQ], in_=Wq.rearrange("(h o) c -> o h c", h=2))
+        nc.sync.dma_start(out=w_rows_view[:, WK], in_=Wk.rearrange("(h o) c -> o h c", h=2))
+        nc.vector.memset(bias_rows[:], 0.0)
+        nc.sync.dma_start(out=bias_rows[0:1, :C8], in_=bq.rearrange("(a o) -> a o", a=1))
+        nc.sync.dma_start(out=bias_rows[0:1, C8:], in_=bk.rearrange("(a o) -> a o", a=1))
+        for n in range(1, RAW_BUFS):
+            load(n)
+        nc.vector.memset(ones[:], 1.0)
+        make_identity(nc, ident[:])
+
+        regroup(0)
+        prepare_weights()
+        for n in range(1, N_PIECES + 3):
+            if n < N_PIECES:
+                regroup(n)
+            if n - 1 < N_PIECES:
+                quantise(n - 1)
+            if 0 <= n - 2 < N_UNITS:
+                multiply(n - 2)
+            if 0 <= n - 3 < N_UNITS:
+                evacuate(n - 3)

@@ -26,7 +26,10 @@ BLOCKS = 2
 RUN = 4
 RUNS = SLAB_PAIRS // RUN
 SCALAR_RUNS = 88
-RAW_BUFS = 8
+CHUNKS = [(0, 1), (1, 1)] + [(slab, 2) for slab in range(2, B * SLABS_PER_IMAGE, 2)]
+CHUNK_SLABS = 2
+N_CHUNKS = len(CHUNKS) * PASSES
+RAW_BUFS = 6
 WQ, WK = 0, 1
 
 FLOPS = 2 * B * H * W * C * 2 * C8
@@ -53,6 +56,7 @@ def tile_selfattention_pb_t_kernel(tc, x, Wq, bq, Wk, bk, out_0, out_1):
         k_psum = ctx.enter_context(tc.psum_pool(name="k_psum", bufs=2))
 
         raw_tiles = {}
+        last_piece = {}
         grouped_tiles = {}
         x_codes = {}
         x_scales = {}
@@ -60,25 +64,29 @@ def tile_selfattention_pb_t_kernel(tc, x, Wq, bq, Wk, bk, out_0, out_1):
         k_banks = {}
         k_stages = {}
 
-        def load(n):
-            slab, g = divmod(n, PASSES)
-            b, s = divmod(slab, SLABS_PER_IMAGE)
-            raw = raw_pool.tile([P, PACK, SLAB_PX], BF16)
+        def load(chunk):
+            first_slab, slabs = CHUNKS[chunk // PASSES]
+            g = chunk % PASSES
+            b, s = divmod(first_slab, SLABS_PER_IMAGE)
+            raw = raw_pool.tile([P, PACK, CHUNK_SLABS * SLAB_PX], BF16)
             nc.sync.dma_start(
-                out=raw[:], in_=x_view[b, g, :, :, s * SLAB_PX : (s + 1) * SLAB_PX]
+                out=raw[:, :, : slabs * SLAB_PX],
+                in_=x_view[b, g, :, :, s * SLAB_PX : (s + slabs) * SLAB_PX],
             )
-            raw_tiles[n] = raw
+            for i in range(slabs):
+                raw_tiles[(first_slab + i) * PASSES + g] = raw[:, :, i * SLAB_PX : (i + 1) * SLAB_PX]
+            last_piece[(first_slab + slabs - 1) * PASSES + g] = chunk
 
         def regroup(n):
-            src = raw_tiles[n][:].rearrange("p j (c i d) -> p d c j i", i=RUN, d=2)
+            src = raw_tiles[n].rearrange("p j (c i d) -> p d c j i", i=RUN, d=2)
             grouped = grouped_pool.tile([P, 2, SLAB_PAIRS, PACK], BF16, align_bytes=64)
             dst = grouped[:].rearrange("p d (c i) j -> p d c j i", i=RUN)
             for d in range(2):
                 nc.scalar.copy(out=dst[:, d, :SCALAR_RUNS], in_=src[:, d, :SCALAR_RUNS])
                 nc.vector.tensor_copy(out=dst[:, d, SCALAR_RUNS:], in_=src[:, d, SCALAR_RUNS:])
             grouped_tiles[n] = grouped
-            if n + RAW_BUFS < N_PIECES:
-                load(n + RAW_BUFS)
+            if n in last_piece and last_piece[n] + RAW_BUFS < N_CHUNKS:
+                load(last_piece[n] + RAW_BUFS)
 
         def quantise(n):
             codes = codes_pool.tile([P, 2 * SLAB_PAIRS], U32, align_bytes=64)

@@ -25,11 +25,11 @@ N_UNITS = B * SLABS_PER_IMAGE * 2
 BLOCKS = 2
 RUN = 4
 RUNS = SLAB_PAIRS // RUN
-SCALAR_RUNS = 88
-CHUNKS = [(0, 1), (1, 1)] + [(slab, 2) for slab in range(2, B * SLABS_PER_IMAGE, 2)]
-CHUNK_SLABS = 2
-N_CHUNKS = len(CHUNKS) * PASSES
-RAW_BUFS = 6
+SCALAR_RUNS = 80
+GPSIMD_RUNS = 32
+FILL_PIECES = 3
+FILL_SCALAR_RUNS = 64
+RAW_BUFS = 8
 WQ, WK = 0, 1
 
 FLOPS = 2 * B * H * W * C * 2 * C8
@@ -51,12 +51,10 @@ def tile_selfattention_pb_t_kernel(tc, x, Wq, bq, Wk, bk, out_0, out_1):
         q_stage_pool = ctx.enter_context(tc.tile_pool(name="q_stage", bufs=8))
         k_stage_pool = ctx.enter_context(tc.tile_pool(name="k_stage", bufs=4))
         even_pool = ctx.enter_context(tc.tile_pool(name="even", bufs=2))
-        setup_psum = ctx.enter_context(tc.psum_pool(name="setup_psum", bufs=2))
         q_psum = ctx.enter_context(tc.psum_pool(name="q_psum", bufs=2 * BLOCKS))
-        k_psum = ctx.enter_context(tc.psum_pool(name="k_psum", bufs=2))
+        k_psum = ctx.enter_context(tc.psum_pool(name="k_psum", bufs=4))
 
         raw_tiles = {}
-        last_piece = {}
         grouped_tiles = {}
         x_codes = {}
         x_scales = {}
@@ -64,29 +62,36 @@ def tile_selfattention_pb_t_kernel(tc, x, Wq, bq, Wk, bk, out_0, out_1):
         k_banks = {}
         k_stages = {}
 
-        def load(chunk):
-            first_slab, slabs = CHUNKS[chunk // PASSES]
-            g = chunk % PASSES
-            b, s = divmod(first_slab, SLABS_PER_IMAGE)
-            raw = raw_pool.tile([P, PACK, CHUNK_SLABS * SLAB_PX], BF16)
+        def load(n):
+            slab, g = divmod(n, PASSES)
+            b, s = divmod(slab, SLABS_PER_IMAGE)
+            raw = raw_pool.tile([P, PACK, SLAB_PX], BF16)
             nc.sync.dma_start(
-                out=raw[:, :, : slabs * SLAB_PX],
-                in_=x_view[b, g, :, :, s * SLAB_PX : (s + slabs) * SLAB_PX],
+                out=raw[:], in_=x_view[b, g, :, :, s * SLAB_PX : (s + 1) * SLAB_PX]
             )
-            for i in range(slabs):
-                raw_tiles[(first_slab + i) * PASSES + g] = raw[:, :, i * SLAB_PX : (i + 1) * SLAB_PX]
-            last_piece[(first_slab + slabs - 1) * PASSES + g] = chunk
+            raw_tiles[n] = raw
 
         def regroup(n):
-            src = raw_tiles[n].rearrange("p j (c i d) -> p d c j i", i=RUN, d=2)
+            src = raw_tiles[n][:].rearrange("p j (c i d) -> p d c j i", i=RUN, d=2)
             grouped = grouped_pool.tile([P, 2, SLAB_PAIRS, PACK], BF16, align_bytes=64)
             dst = grouped[:].rearrange("p d (c i) j -> p d c j i", i=RUN)
+            cut = FILL_SCALAR_RUNS if n < FILL_PIECES else SCALAR_RUNS
             for d in range(2):
-                nc.scalar.copy(out=dst[:, d, :SCALAR_RUNS], in_=src[:, d, :SCALAR_RUNS])
-                nc.vector.tensor_copy(out=dst[:, d, SCALAR_RUNS:], in_=src[:, d, SCALAR_RUNS:])
+                nc.scalar.copy(out=dst[:, d, :cut], in_=src[:, d, :cut])
+                nc.gpsimd.tensor_scalar(
+                    out=dst[:, d, cut : cut + GPSIMD_RUNS],
+                    in0=src[:, d, cut : cut + GPSIMD_RUNS],
+                    scalar1=1.0,
+                    scalar2=0.0,
+                    op0=MULT,
+                    op1=ADD,
+                )
+                nc.vector.tensor_copy(
+                    out=dst[:, d, cut + GPSIMD_RUNS :], in_=src[:, d, cut + GPSIMD_RUNS :]
+                )
             grouped_tiles[n] = grouped
-            if n in last_piece and last_piece[n] + RAW_BUFS < N_CHUNKS:
-                load(last_piece[n] + RAW_BUFS)
+            if n + RAW_BUFS < N_PIECES:
+                load(n + RAW_BUFS)
 
         def quantise(n):
             codes = codes_pool.tile([P, 2 * SLAB_PAIRS], U32, align_bytes=64)
@@ -108,19 +113,19 @@ def tile_selfattention_pb_t_kernel(tc, x, Wq, bq, Wk, bk, out_0, out_1):
             )
             for w in range(2):
                 for g in range(PASSES):
-                    planes = setup_psum.tile([P, 2, C8], F32, tag="setup")
+                    planes = q_psum.tile([P, 2, C8], F32, tag="q_ps")
                     for u in range(2):
                         for h in range(2):
                             nc.tensor.transpose(
                                 planes[:, u, h * P : (h + 1) * P], w_words[:, w, h, g, u, :], ident[:]
                             )
-                    nc.scalar.copy(
+                    nc.vector.tensor_copy(
                         out=grouped_words[:, w, g], in_=planes[:].rearrange("p u o -> p o u")
                     )
             nc.vector.quantize_mx(
                 out=w_codes[:].bitcast(FP8X4), scales=w_scales[:], in_=w_grouped[:]
             )
-            spread = setup_psum.tile([P, C8 + 2 * 32], F32, tag="setup")
+            spread = q_psum.tile([P, C8 + 2 * 32], F32, tag="q_ps")
             nc.tensor.matmul(
                 out=spread[:, :C8], lhsT=ones[:], rhs=bias_rows[:, :C8], start=True, stop=True
             )
@@ -137,7 +142,24 @@ def tile_selfattention_pb_t_kernel(tc, x, Wq, bq, Wk, bk, out_0, out_1):
                 out=bias_k[:], in_=spread[:, C8:].rearrange("p (h n) -> p h n", h=2)[:, :, 0]
             )
 
-        def multiply(unit):
+        def multiply_k(n):
+            slab, g = divmod(n, PASSES)
+            for half in range(2):
+                if g == 0:
+                    k_ps = k_psum.tile([P, SLAB_PAIRS], F32)
+                    k_banks[slab * 2 + half] = k_ps
+                for d in range(2):
+                    nc.tensor.matmul_mx(
+                        out=k_banks[slab * 2 + half][:],
+                        lhsT=w_codes_view[:, WK, g, half * P : (half + 1) * P].bitcast(FP8X4),
+                        lhsT_scale=w_scales_view[:, WK, g, half * P : (half + 1) * P],
+                        rhs=x_codes[n][:, d * SLAB_PAIRS : (d + 1) * SLAB_PAIRS].bitcast(FP8X4),
+                        rhs_scale=x_scales[n][:, d * SLAB_PAIRS : (d + 1) * SLAB_PAIRS],
+                        start=(g == 0 and d == 0),
+                        stop=(g == PASSES - 1 and d == 1),
+                    )
+
+        def multiply_q(unit):
             slab, half = divmod(unit, 2)
             pieces = [slab * PASSES + g for g in range(PASSES)]
             q_banks[unit] = []
@@ -156,19 +178,6 @@ def tile_selfattention_pb_t_kernel(tc, x, Wq, bq, Wk, bk, out_0, out_1):
                             stop=(g == PASSES - 1),
                         )
                 q_banks[unit].append(q_ps)
-            k_ps = k_psum.tile([P, SLAB_PAIRS], F32)
-            for d in range(2):
-                for g in range(PASSES):
-                    nc.tensor.matmul_mx(
-                        out=k_ps[:],
-                        lhsT=w_codes_view[:, WK, g, half * P : (half + 1) * P].bitcast(FP8X4),
-                        lhsT_scale=w_scales_view[:, WK, g, half * P : (half + 1) * P],
-                        rhs=x_codes[pieces[g]][:, d * SLAB_PAIRS : (d + 1) * SLAB_PAIRS].bitcast(FP8X4),
-                        rhs_scale=x_scales[pieces[g]][:, d * SLAB_PAIRS : (d + 1) * SLAB_PAIRS],
-                        start=(d == 0 and g == 0),
-                        stop=(d == 1 and g == PASSES - 1),
-                    )
-            k_banks[unit] = k_ps
 
         def evacuate(unit):
             slab, half = divmod(unit, 2)
@@ -236,7 +245,8 @@ def tile_selfattention_pb_t_kernel(tc, x, Wq, bq, Wk, bk, out_0, out_1):
                 regroup(n)
             if n - 1 < N_PIECES:
                 quantise(n - 1)
+                multiply_k(n - 1)
             if 0 <= n - 2 < N_UNITS:
-                multiply(n - 2)
+                multiply_q(n - 2)
             if 0 <= n - 3 < N_UNITS:
                 evacuate(n - 3)

@@ -16,20 +16,22 @@ B, C, C8, H, W = 2, 1024, 256, 64, 64
 P = 128
 PACK = 4
 PASSES = C // (P * PACK)
-SLAB_ROWS = 16
-SLAB_PX = SLAB_ROWS * W
-SLAB_PAIRS = SLAB_PX // 2
-SLABS_PER_IMAGE = H // SLAB_ROWS
-N_PIECES = B * SLABS_PER_IMAGE * PASSES
-N_UNITS = B * SLABS_PER_IMAGE * 2
-BLOCKS = 2
+UNIT_ROWS = 8
+UNIT_PX = UNIT_ROWS * W
+UNIT_PAIRS = UNIT_PX // 2
+UNITS_PER_IMAGE = H // UNIT_ROWS
+BLOCKS = UNIT_PAIRS // P
+POOLED = UNIT_PAIRS // 2
+SLAB_UNITS = [1, 1, 2, 2, 2, 2, 2, 2, 1, 1]
+SLAB_FIRST = [sum(SLAB_UNITS[:i]) for i in range(len(SLAB_UNITS))]
+N_PIECES = len(SLAB_UNITS) * PASSES
 RUN = 4
-RUNS = SLAB_PAIRS // RUN
-SCALAR_RUNS = 80
-GPSIMD_RUNS = 32
-FILL_PIECES = 3
-FILL_SCALAR_RUNS = 64
+SCALAR_RUNS = 40
+GPSIMD_RUNS = 16
+FILL_PIECES = 5
+FILL_SCALAR_RUNS = 32
 RAW_BUFS = 8
+K_STORES = {(0, 7): (0, 8), (1, 5): (0, 6), (1, 7): (6, 8)}
 WQ, WK = 0, 1
 
 FLOPS = 2 * B * H * W * C * 2 * C8
@@ -39,9 +41,9 @@ def tile_selfattention_pb_t_kernel(tc, x, Wq, bq, Wk, bk, out_0, out_1):
     nc = tc.nc
     x_view = x.rearrange("b (g p j) h w -> b g p j (h w)", g=PASSES, p=P, j=PACK)
     q_view = out_0.rearrange(
-        "b (u k p d) o -> b u p k (d o)", u=2 * SLABS_PER_IMAGE, k=BLOCKS, p=P, d=2
+        "b (u k p d) o -> b u p k (d o)", u=UNITS_PER_IMAGE, k=BLOCKS, p=P, d=2
     )
-    k_view = out_1.rearrange("b (h o) t -> b h o t", h=2)
+    k_view = out_1.rearrange("b (h o) t -> b o h t", h=2)
 
     with ExitStack() as ctx:
         const = ctx.enter_context(tc.tile_pool(name="const", bufs=1))
@@ -49,10 +51,10 @@ def tile_selfattention_pb_t_kernel(tc, x, Wq, bq, Wk, bk, out_0, out_1):
         grouped_pool = ctx.enter_context(tc.tile_pool(name="grouped", bufs=3))
         codes_pool = ctx.enter_context(tc.tile_pool(name="codes", bufs=6))
         q_stage_pool = ctx.enter_context(tc.tile_pool(name="q_stage", bufs=8))
-        k_stage_pool = ctx.enter_context(tc.tile_pool(name="k_stage", bufs=4))
+        k_stage_pool = ctx.enter_context(tc.tile_pool(name="k_stage", bufs=2))
         even_pool = ctx.enter_context(tc.tile_pool(name="even", bufs=2))
-        q_psum = ctx.enter_context(tc.psum_pool(name="q_psum", bufs=2 * BLOCKS))
-        k_psum = ctx.enter_context(tc.psum_pool(name="k_psum", bufs=4))
+        q_psum = ctx.enter_context(tc.psum_pool(name="q_psum", bufs=5))
+        k_psum = ctx.enter_context(tc.psum_pool(name="k_psum", bufs=3))
 
         raw_tiles = {}
         grouped_tiles = {}
@@ -62,40 +64,45 @@ def tile_selfattention_pb_t_kernel(tc, x, Wq, bq, Wk, bk, out_0, out_1):
         k_banks = {}
         k_stages = {}
 
+        def pairs_of(n):
+            return SLAB_UNITS[n // PASSES] * UNIT_PAIRS
+
         def load(n):
             slab, g = divmod(n, PASSES)
-            b, s = divmod(slab, SLABS_PER_IMAGE)
-            raw = raw_pool.tile([P, PACK, SLAB_PX], BF16)
+            b, u = divmod(SLAB_FIRST[slab], UNITS_PER_IMAGE)
+            raw = raw_pool.tile([P, PACK, 2 * pairs_of(n)], BF16)
             nc.sync.dma_start(
-                out=raw[:], in_=x_view[b, g, :, :, s * SLAB_PX : (s + 1) * SLAB_PX]
+                out=raw[:],
+                in_=x_view[b, g, :, :, u * UNIT_PX : u * UNIT_PX + 2 * pairs_of(n)],
             )
             raw_tiles[n] = raw
 
         def regroup(n):
             src = raw_tiles[n][:].rearrange("p j (c i d) -> p d c j i", i=RUN, d=2)
-            grouped = grouped_pool.tile([P, 2, SLAB_PAIRS, PACK], BF16, align_bytes=64)
+            grouped = grouped_pool.tile([P, 2, pairs_of(n), PACK], BF16, align_bytes=64)
             dst = grouped[:].rearrange("p d (c i) j -> p d c j i", i=RUN)
-            cut = FILL_SCALAR_RUNS if n < FILL_PIECES else SCALAR_RUNS
+            units = SLAB_UNITS[n // PASSES]
+            cut = units * (FILL_SCALAR_RUNS if n < FILL_PIECES else SCALAR_RUNS)
+            cut_2 = cut + units * GPSIMD_RUNS
             for d in range(2):
                 nc.scalar.copy(out=dst[:, d, :cut], in_=src[:, d, :cut])
                 nc.gpsimd.tensor_scalar(
-                    out=dst[:, d, cut : cut + GPSIMD_RUNS],
-                    in0=src[:, d, cut : cut + GPSIMD_RUNS],
+                    out=dst[:, d, cut:cut_2],
+                    in0=src[:, d, cut:cut_2],
                     scalar1=1.0,
                     scalar2=0.0,
                     op0=MULT,
                     op1=ADD,
                 )
-                nc.vector.tensor_copy(
-                    out=dst[:, d, cut + GPSIMD_RUNS :], in_=src[:, d, cut + GPSIMD_RUNS :]
-                )
+                nc.vector.tensor_copy(out=dst[:, d, cut_2:], in_=src[:, d, cut_2:])
             grouped_tiles[n] = grouped
             if n + RAW_BUFS < N_PIECES:
                 load(n + RAW_BUFS)
 
         def quantise(n):
-            codes = codes_pool.tile([P, 2 * SLAB_PAIRS], U32, align_bytes=64)
-            scales = codes_pool.tile([P, 2 * SLAB_PAIRS], U8, align_bytes=64)
+            columns = 2 * pairs_of(n)
+            codes = codes_pool.tile([P, columns], U32, align_bytes=64)
+            scales = codes_pool.tile([P, columns], U8, align_bytes=64)
             nc.vector.quantize_mx(
                 out=codes[:].bitcast(FP8X4),
                 scales=scales[:],
@@ -142,36 +149,26 @@ def tile_selfattention_pb_t_kernel(tc, x, Wq, bq, Wk, bk, out_0, out_1):
                 out=bias_k[:], in_=spread[:, C8:].rearrange("p (h n) -> p h n", h=2)[:, :, 0]
             )
 
-        def multiply_k(n):
-            slab, g = divmod(n, PASSES)
-            for half in range(2):
-                if g == 0:
-                    k_ps = k_psum.tile([P, SLAB_PAIRS], F32)
-                    k_banks[slab * 2 + half] = k_ps
-                for d in range(2):
-                    nc.tensor.matmul_mx(
-                        out=k_banks[slab * 2 + half][:],
-                        lhsT=w_codes_view[:, WK, g, half * P : (half + 1) * P].bitcast(FP8X4),
-                        lhsT_scale=w_scales_view[:, WK, g, half * P : (half + 1) * P],
-                        rhs=x_codes[n][:, d * SLAB_PAIRS : (d + 1) * SLAB_PAIRS].bitcast(FP8X4),
-                        rhs_scale=x_scales[n][:, d * SLAB_PAIRS : (d + 1) * SLAB_PAIRS],
-                        start=(g == 0 and d == 0),
-                        stop=(g == PASSES - 1 and d == 1),
-                    )
+        def x_window(slab, g, d, first, count):
+            n = slab * PASSES + g
+            begin = d * pairs_of(n) + first
+            return (
+                x_codes[n][:, begin : begin + count].bitcast(FP8X4),
+                x_scales[n][:, begin : begin + count],
+            )
 
-        def multiply_q(unit):
-            slab, half = divmod(unit, 2)
-            pieces = [slab * PASSES + g for g in range(PASSES)]
+        def multiply_q(slab, part):
+            unit = SLAB_FIRST[slab] + part
             q_banks[unit] = []
             for k in range(BLOCKS):
                 q_ps = q_psum.tile([P, 2, C8], F32)
                 for d in range(2):
-                    first = d * SLAB_PAIRS + (half * BLOCKS + k) * P
                     for g in range(PASSES):
+                        codes, scales = x_window(slab, g, d, part * UNIT_PAIRS + k * P, P)
                         nc.tensor.matmul_mx(
                             out=q_ps[:, d, :],
-                            lhsT=x_codes[pieces[g]][:, first : first + P].bitcast(FP8X4),
-                            lhsT_scale=x_scales[pieces[g]][:, first : first + P],
+                            lhsT=codes,
+                            lhsT_scale=scales,
                             rhs=w_codes_view[:, WQ, g, :].bitcast(FP8X4),
                             rhs_scale=w_scales_view[:, WQ, g, :],
                             start=(g == 0),
@@ -179,15 +176,38 @@ def tile_selfattention_pb_t_kernel(tc, x, Wq, bq, Wk, bk, out_0, out_1):
                         )
                 q_banks[unit].append(q_ps)
 
+        def multiply_k(slab, part):
+            unit = SLAB_FIRST[slab] + part
+            k_ps = k_psum.tile([P, 2, UNIT_PAIRS], F32)
+            for half in range(2):
+                for g in range(PASSES):
+                    for d in range(2):
+                        codes, scales = x_window(slab, g, d, part * UNIT_PAIRS, UNIT_PAIRS)
+                        nc.tensor.matmul_mx(
+                            out=k_ps[:, half, :],
+                            lhsT=w_codes_view[:, WK, g, half * P : (half + 1) * P].bitcast(FP8X4),
+                            lhsT_scale=w_scales_view[:, WK, g, half * P : (half + 1) * P],
+                            rhs=codes,
+                            rhs_scale=scales,
+                            start=(g == 0 and d == 0),
+                            stop=(g == PASSES - 1 and d == 1),
+                        )
+            k_banks[unit] = k_ps
+
         def evacuate(unit):
-            slab, half = divmod(unit, 2)
-            b, s = divmod(slab, SLABS_PER_IMAGE)
-            rows = k_banks[unit][:].rearrange("o (m e n) -> o e m n", e=2, n=W // 2)
-            even = even_pool.tile([P, SLAB_ROWS // 2, W // 2], F32)
-            nc.scalar.activation(
-                out=even[:], in_=rows[:, 0], func=IDENTITY, bias=bias_k[:, half : half + 1], scale=0.25
-            )
+            b, u = divmod(unit, UNITS_PER_IMAGE)
+            rows = k_banks[unit][:].rearrange("o h (m e n) -> o h e m n", e=2, n=W // 2)
+            even = even_pool.tile([P, 2, UNIT_ROWS // 2, W // 2], F32)
+            for half in range(2):
+                nc.scalar.activation(
+                    out=even[:, half],
+                    in_=rows[:, half, 0],
+                    func=IDENTITY,
+                    bias=bias_k[:, half : half + 1],
+                    scale=0.25,
+                )
             q_stage = q_stage_pool.tile([P, BLOCKS, 2, C8], F32)
+            last = unit == B * UNITS_PER_IMAGE - 1
             for k in range(BLOCKS):
                 nc.vector.tensor_tensor(
                     out=q_stage[:, k],
@@ -195,23 +215,31 @@ def tile_selfattention_pb_t_kernel(tc, x, Wq, bq, Wk, bk, out_0, out_1):
                     in1=bias_q[:].unsqueeze(1).to_broadcast([P, 2, C8]),
                     op=ADD,
                 )
-            nc.sync.dma_start(
-                out=q_view[b, s * 2 + half], in_=q_stage[:].rearrange("p k d o -> p k (d o)")
-            )
-            if s == 0:
-                k_stage = k_stage_pool.tile([P, SLABS_PER_IMAGE, SLAB_ROWS // 2, W // 2], F32)
-                k_stages[(b, half)] = k_stage
+                if last:
+                    nc.sync.dma_start(
+                        out=q_view[b, u, :, k], in_=q_stage[:, k].rearrange("p d o -> p (d o)")
+                    )
+            if not last:
+                nc.sync.dma_start(
+                    out=q_view[b, u], in_=q_stage[:].rearrange("p k d o -> p k (d o)")
+                )
+            if u == 0:
+                k_stages[b] = k_stage_pool.tile([P, 2, UNITS_PER_IMAGE * POOLED], F32, name="k_stage")
             nc.vector.scalar_tensor_tensor(
-                out=k_stages[(b, half)][:, s],
-                in0=rows[:, 1],
+                out=k_stages[b][:, :, u * POOLED : (u + 1) * POOLED].rearrange(
+                    "o h (m n) -> o h m n", n=W // 2
+                ),
+                in0=rows[:, :, 1],
                 scalar=0.25,
                 in1=even[:],
                 op0=MULT,
                 op1=ADD,
             )
-            if s == SLABS_PER_IMAGE - 1:
+            if (b, u) in K_STORES:
+                first, end = K_STORES[(b, u)]
                 nc.sync.dma_start(
-                    out=k_view[b, half], in_=k_stages[(b, half)][:].rearrange("o s m n -> o (s m n)")
+                    out=k_view[b, :, :, first * POOLED : end * POOLED],
+                    in_=k_stages[b][:, :, first * POOLED : end * POOLED],
                 )
 
         w_rows = const.tile([P, 2 * 2 * C], BF16)
@@ -238,6 +266,8 @@ def tile_selfattention_pb_t_kernel(tc, x, Wq, bq, Wk, bk, out_0, out_1):
         nc.vector.memset(ones[:], 1.0)
         make_identity(nc, ident[:])
 
+        ready = []
+        multiplied = []
         regroup(0)
         prepare_weights()
         for n in range(1, N_PIECES + 3):
@@ -245,8 +275,16 @@ def tile_selfattention_pb_t_kernel(tc, x, Wq, bq, Wk, bk, out_0, out_1):
                 regroup(n)
             if n - 1 < N_PIECES:
                 quantise(n - 1)
-                multiply_k(n - 1)
-            if 0 <= n - 2 < N_UNITS:
-                multiply_q(n - 2)
-            if 0 <= n - 3 < N_UNITS:
-                evacuate(n - 3)
+                slab, g = divmod(n - 1, PASSES)
+                if g == PASSES - 1:
+                    ready.extend([(slab, part) for part in range(SLAB_UNITS[slab])])
+            done = list(multiplied)
+            multiplied.clear()
+            if ready:
+                slab, part = ready[0]
+                ready.remove((slab, part))
+                multiply_q(slab, part)
+                multiply_k(slab, part)
+                multiplied.extend([SLAB_FIRST[slab] + part])
+            for unit in done:
+                evacuate(unit)

from contextlib import ExitStack

import concourse.mybir as mybir
from concourse.masks import make_identity

BF16 = mybir.dt.bfloat16
F32 = mybir.dt.float32
U32 = mybir.dt.uint32
U8 = mybir.dt.uint8
FP8X4 = mybir.dt.float8_e4m3fn_x4
ADD = mybir.AluOpType.add
MULT = mybir.AluOpType.mult
IDENTITY = mybir.ActivationFunctionType.Identity

B, C, C8, H, W = 2, 1024, 256, 64, 64
P = 128
PACK = 4
PASSES = C // (P * PACK)
UNIT_ROWS = 8
UNIT_PX = UNIT_ROWS * W
UNIT_PAIRS = UNIT_PX // 2
UNITS_PER_IMAGE = H // UNIT_ROWS
BLOCKS = UNIT_PAIRS // P
POOLED = UNIT_PAIRS // 2
SLAB_UNITS = [1, 1, 2, 2, 2, 2, 2, 2, 1, 1]
SLAB_FIRST = [sum(SLAB_UNITS[:i]) for i in range(len(SLAB_UNITS))]
N_PIECES = len(SLAB_UNITS) * PASSES
RUN = 4
SCALAR_RUNS = 40
GPSIMD_RUNS = 16
FILL_PIECES = 5
FILL_SCALAR_RUNS = 32
RAW_BUFS = 8
K_STORES = {(0, 7): (0, 8), (1, 5): (0, 6), (1, 7): (6, 8)}
WQ, WK = 0, 1

FLOPS = 2 * B * H * W * C * 2 * C8


def tile_selfattention_pb_t_kernel(tc, x, Wq, bq, Wk, bk, out_0, out_1):
    nc = tc.nc
    x_view = x.rearrange("b (g p j) h w -> b g p j (h w)", g=PASSES, p=P, j=PACK)
    q_view = out_0.rearrange(
        "b (u k p d) o -> b u p k (d o)", u=UNITS_PER_IMAGE, k=BLOCKS, p=P, d=2
    )
    k_view = out_1.rearrange("b (h o) t -> b o h t", h=2)

    with ExitStack() as ctx:
        const = ctx.enter_context(tc.tile_pool(name="const", bufs=1))
        raw_pool = ctx.enter_context(tc.tile_pool(name="raw", bufs=RAW_BUFS))
        grouped_pool = ctx.enter_context(tc.tile_pool(name="grouped", bufs=3))
        codes_pool = ctx.enter_context(tc.tile_pool(name="codes", bufs=6))
        q_stage_pool = ctx.enter_context(tc.tile_pool(name="q_stage", bufs=8))
        k_stage_pool = ctx.enter_context(tc.tile_pool(name="k_stage", bufs=2))
        even_pool = ctx.enter_context(tc.tile_pool(name="even", bufs=2))
        q_psum = ctx.enter_context(tc.psum_pool(name="q_psum", bufs=5))
        k_psum = ctx.enter_context(tc.psum_pool(name="k_psum", bufs=3))

        raw_tiles = {}
        grouped_tiles = {}
        x_codes = {}
        x_scales = {}
        q_banks = {}
        k_banks = {}
        k_stages = {}

        def pairs_of(n):
            return SLAB_UNITS[n // PASSES] * UNIT_PAIRS

        def load(n):
            slab, g = divmod(n, PASSES)
            b, u = divmod(SLAB_FIRST[slab], UNITS_PER_IMAGE)
            raw = raw_pool.tile([P, PACK, 2 * pairs_of(n)], BF16)
            nc.sync.dma_start(
                out=raw[:],
                in_=x_view[b, g, :, :, u * UNIT_PX : u * UNIT_PX + 2 * pairs_of(n)],
            )
            raw_tiles[n] = raw

        def regroup(n):
            src = raw_tiles[n][:].rearrange("p j (c i d) -> p d c j i", i=RUN, d=2)
            grouped = grouped_pool.tile([P, 2, pairs_of(n), PACK], BF16, align_bytes=64)
            dst = grouped[:].rearrange("p d (c i) j -> p d c j i", i=RUN)
            units = SLAB_UNITS[n // PASSES]
            cut = units * (FILL_SCALAR_RUNS if n < FILL_PIECES else SCALAR_RUNS)
            cut_2 = cut + units * GPSIMD_RUNS
            for d in range(2):
                nc.scalar.copy(out=dst[:, d, :cut], in_=src[:, d, :cut])
                nc.gpsimd.tensor_scalar(
                    out=dst[:, d, cut:cut_2],
                    in0=src[:, d, cut:cut_2],
                    scalar1=1.0,
                    scalar2=0.0,
                    op0=MULT,
                    op1=ADD,
                )
                nc.vector.tensor_copy(out=dst[:, d, cut_2:], in_=src[:, d, cut_2:])
            grouped_tiles[n] = grouped
            if n + RAW_BUFS < N_PIECES:
                load(n + RAW_BUFS)

        def quantise(n):
            columns = 2 * pairs_of(n)
            codes = codes_pool.tile([P, columns], U32, align_bytes=64)
            scales = codes_pool.tile([P, columns], U8, align_bytes=64)
            nc.vector.quantize_mx(
                out=codes[:].bitcast(FP8X4),
                scales=scales[:],
                in_=grouped_tiles[n][:].rearrange("p d q j -> p (d q j)"),
            )
            x_codes[n] = codes
            x_scales[n] = scales

        def prepare_weights():
            w_words = w_rows[:].bitcast(F32).rearrange(
                "o (w h g p u) -> o w h g u p", w=2, h=2, g=PASSES, p=P, u=2
            )
            grouped_words = w_grouped[:].bitcast(F32).rearrange(
                "p (w g o u) -> p w g o u", w=2, g=PASSES, o=C8, u=2
            )
            for w in range(2):
                for g in range(PASSES):
                    planes = q_psum.tile([P, 2, C8], F32, tag="q_ps")
                    for u in range(2):
                        for h in range(2):
                            nc.tensor.transpose(
                                planes[:, u, h * P : (h + 1) * P], w_words[:, w, h, g, u, :], ident[:]
                            )
                    nc.vector.tensor_copy(
                        out=grouped_words[:, w, g], in_=planes[:].rearrange("p u o -> p o u")
                    )
            nc.vector.quantize_mx(
                out=w_codes[:].bitcast(FP8X4), scales=w_scales[:], in_=w_grouped[:]
            )
            spread = q_psum.tile([P, C8 + 2 * 32], F32, tag="q_ps")
            nc.tensor.matmul(
                out=spread[:, :C8], lhsT=ones[:], rhs=bias_rows[:, :C8], start=True, stop=True
            )
            for h in range(2):
                nc.tensor.matmul(
                    out=spread[:, C8 + 32 * h : C8 + 32 * (h + 1)],
                    lhsT=bias_rows[:, C8 + h * P : C8 + (h + 1) * P],
                    rhs=ones[:, :32],
                    start=True,
                    stop=True,
                )
            nc.vector.tensor_copy(out=bias_q[:], in_=spread[:, :C8])
            nc.vector.tensor_copy(
                out=bias_k[:], in_=spread[:, C8:].rearrange("p (h n) -> p h n", h=2)[:, :, 0]
            )

        def x_window(slab, g, d, first, count):
            n = slab * PASSES + g
            begin = d * pairs_of(n) + first
            return (
                x_codes[n][:, begin : begin + count].bitcast(FP8X4),
                x_scales[n][:, begin : begin + count],
            )

        def multiply_q(slab, part):
            unit = SLAB_FIRST[slab] + part
            q_banks[unit] = []
            for k in range(BLOCKS):
                q_ps = q_psum.tile([P, 2, C8], F32)
                for d in range(2):
                    for g in range(PASSES):
                        codes, scales = x_window(slab, g, d, part * UNIT_PAIRS + k * P, P)
                        nc.tensor.matmul_mx(
                            out=q_ps[:, d, :],
                            lhsT=codes,
                            lhsT_scale=scales,
                            rhs=w_codes_view[:, WQ, g, :].bitcast(FP8X4),
                            rhs_scale=w_scales_view[:, WQ, g, :],
                            start=(g == 0),
                            stop=(g == PASSES - 1),
                        )
                q_banks[unit].append(q_ps)

        def multiply_k(slab, part):
            unit = SLAB_FIRST[slab] + part
            k_ps = k_psum.tile([P, 2, UNIT_PAIRS], F32)
            for half in range(2):
                for g in range(PASSES):
                    for d in range(2):
                        codes, scales = x_window(slab, g, d, part * UNIT_PAIRS, UNIT_PAIRS)
                        nc.tensor.matmul_mx(
                            out=k_ps[:, half, :],
                            lhsT=w_codes_view[:, WK, g, half * P : (half + 1) * P].bitcast(FP8X4),
                            lhsT_scale=w_scales_view[:, WK, g, half * P : (half + 1) * P],
                            rhs=codes,
                            rhs_scale=scales,
                            start=(g == 0 and d == 0),
                            stop=(g == PASSES - 1 and d == 1),
                        )
            k_banks[unit] = k_ps

        def evacuate(unit):
            b, u = divmod(unit, UNITS_PER_IMAGE)
            rows = k_banks[unit][:].rearrange("o h (m e n) -> o h e m n", e=2, n=W // 2)
            even = even_pool.tile([P, 2, UNIT_ROWS // 2, W // 2], F32)
            for half in range(2):
                nc.scalar.activation(
                    out=even[:, half],
                    in_=rows[:, half, 0],
                    func=IDENTITY,
                    bias=bias_k[:, half : half + 1],
                    scale=0.25,
                )
            q_stage = q_stage_pool.tile([P, BLOCKS, 2, C8], F32)
            last = unit == B * UNITS_PER_IMAGE - 1
            for k in range(BLOCKS):
                nc.vector.tensor_tensor(
                    out=q_stage[:, k],
                    in0=q_banks[unit][k][:],
                    in1=bias_q[:].unsqueeze(1).to_broadcast([P, 2, C8]),
                    op=ADD,
                )
                if last:
                    nc.sync.dma_start(
                        out=q_view[b, u, :, k], in_=q_stage[:, k].rearrange("p d o -> p (d o)")
                    )
            if not last:
                nc.sync.dma_start(
                    out=q_view[b, u], in_=q_stage[:].rearrange("p k d o -> p k (d o)")
                )
            if u == 0:
                k_stages[b] = k_stage_pool.tile([P, 2, UNITS_PER_IMAGE * POOLED], F32, name="k_stage")
            nc.vector.scalar_tensor_tensor(
                out=k_stages[b][:, :, u * POOLED : (u + 1) * POOLED].rearrange(
                    "o h (m n) -> o h m n", n=W // 2
                ),
                in0=rows[:, :, 1],
                scalar=0.25,
                in1=even[:],
                op0=MULT,
                op1=ADD,
            )
            if (b, u) in K_STORES:
                first, end = K_STORES[(b, u)]
                nc.sync.dma_start(
                    out=k_view[b, :, :, first * POOLED : end * POOLED],
                    in_=k_stages[b][:, :, first * POOLED : end * POOLED],
                )

        w_rows = const.tile([P, 2 * 2 * C], BF16)
        w_grouped = const.tile([P, 2 * PASSES * C8 * PACK], BF16, align_bytes=64)
        w_codes = const.tile([P, 2 * PASSES * C8], U32, align_bytes=64)
        w_scales = const.tile([P, 2 * PASSES * C8], U8, align_bytes=64)
        w_codes_view = w_codes[:].rearrange("p (w g o) -> p w g o", w=2, g=PASSES)
        w_scales_view = w_scales[:].rearrange("p (w g o) -> p w g o", w=2, g=PASSES)
        bias_rows = const.tile([P, 2 * C8], BF16)
        bias_q = const.tile([P, C8], F32)
        bias_k = const.tile([P, 2], F32)
        ones = const.tile([P, P], BF16)
        ident = const.tile([P, P], F32)

        load(0)
        w_rows_view = w_rows[:].rearrange("o (w h c) -> o w h c", w=2, h=2)
        nc.sync.dma_start(out=w_rows_view[:, WQ], in_=Wq.rearrange("(h o) c -> o h c", h=2))
        nc.sync.dma_start(out=w_rows_view[:, WK], in_=Wk.rearrange("(h o) c -> o h c", h=2))
        nc.vector.memset(bias_rows[:], 0.0)
        nc.sync.dma_start(out=bias_rows[0:1, :C8], in_=bq.rearrange("(a o) -> a o", a=1))
        nc.sync.dma_start(out=bias_rows[0:1, C8:], in_=bk.rearrange("(a o) -> a o", a=1))
        for n in range(1, RAW_BUFS):
            load(n)
        nc.vector.memset(ones[:], 1.0)
        make_identity(nc, ident[:])

        ready = []
        multiplied = []
        regroup(0)
        prepare_weights()
        for n in range(1, N_PIECES + 3):
            if n < N_PIECES:
                regroup(n)
            if n - 1 < N_PIECES:
                quantise(n - 1)
                slab, g = divmod(n - 1, PASSES)
                if g == PASSES - 1:
                    ready.extend([(slab, part) for part in range(SLAB_UNITS[slab])])
            done = list(multiplied)
            multiplied.clear()
            if ready:
                slab, part = ready[0]
                ready.remove((slab, part))
                multiply_q(slab, part)
                multiply_k(slab, part)
                multiplied.extend([SLAB_FIRST[slab] + part])
            for unit in done:
                evacuate(unit)
